import numpy as np
import ml_dtypes


def mxq(x, axis, fmt="e4m3"):
    dtype, down = {"e4m3": (ml_dtypes.float8_e4m3fn, 7), "e5m2": (ml_dtypes.float8_e5m2, 14)}[fmt]
    v = np.moveaxis(np.asarray(x, np.float32).astype(ml_dtypes.bfloat16).astype(np.float64), axis, -1)
    blocks = v.reshape(v.shape[:-1] + (-1, 32))
    amax = np.abs(blocks).max(-1, keepdims=True)
    byte = np.maximum(np.where(amax > 0, np.frexp(amax)[1] - 1 + 127, 0) - down, 1)
    scale = np.exp2(byte - 127.0)
    codes = (blocks / scale).astype(np.float32).astype(dtype).astype(np.float64)
    return np.moveaxis((codes * scale).reshape(v.shape), -1, axis)


WIDE = False


def mx_kscale(k):
    if not WIDE:
        return np.ones(k)
    levels = np.array([10, -10, 5, -5, 0])
    if k % 512:
        return np.exp2(np.random.permutation(np.resize(levels, k // 32))).repeat(32)
    a = np.empty((k // 512, 16))
    for p in range(k // 512):
        a[p, :8] = np.random.permutation(np.resize(levels, 8))
        for g in range(8):
            far = levels[np.abs(levels - a[p, g]) >= 10]
            a[p, g + 8] = far[np.random.randint(len(far))]
    return np.exp2(a.ravel()).repeat(32)


BF16 = ml_dtypes.bfloat16


def bf(x):
    return np.asarray(x, np.float32).astype(BF16)


def f64(x):
    return np.asarray(x).astype(np.float64)


B, S, HID, NH, DH = 4, 256, 1024, 16, 64
DQ = NH * DH


def setup_inputs():
    s = mx_kscale(DQ)
    y = np.random.standard_normal((B, S, DQ)) * 0.3 * s
    h = np.ascontiguousarray(y.reshape(B, NH, S, DH).transpose(0, 2, 1, 3))
    return {"h_attn": bf(h),
            "Wo": bf(np.random.standard_normal((DQ, HID)) * 1.5 / np.sqrt(DQ) / s[:, None]),
            "bo": bf(np.random.standard_normal(HID) * 0.3)}


def core(h_attn, Wo, bo):
    y = f64(h_attn).transpose(0, 2, 1, 3).reshape(B, -1, DQ)
    return (mxq(y, 2, "e4m3") @ mxq(f64(Wo), 0, "e4m3")) + f64(bo)


def e4m3fn_bytes(y):
    return np.clip(np.asarray(y, np.float64), -448.0, 448.0).astype(np.float32).astype(ml_dtypes.float8_e4m3fn).view(np.uint8)


def reference(h_attn, Wo, bo):
    out = core(h_attn, Wo, bo)
    s = np.max(np.abs(out), axis=-1, keepdims=True) / 448.0
    return out, e4m3fn_bytes(out / s)

@@ -1,0 +1,282 @@
+from contextlib import ExitStack
+
+import concourse.mybir as mybir
+from concourse.masks import make_identity
+
+FLOPS = 2 * 1024 * 1024 * 1024
+
+F32 = mybir.dt.float32
+BF16 = mybir.dt.bfloat16
+U32 = mybir.dt.uint32
+U8 = mybir.dt.uint8
+FP8X4 = mybir.dt.float8_e4m3fn_x4
+FP8 = mybir.dt.float8_e4m3fn
+ALU = mybir.AluOpType
+ACT = mybir.ActivationFunctionType
+AX = mybir.AxisListType
+
+P = 128
+NB = 512
+N = 1024
+TILES = 8
+W_VEC = 336
+LAST_VEC = 672
+BY_POOL = ((3, 1), (5, 1), (6, 1))
+Y1_STEP = 3
+
+
+def tile_reasoningmultiheadattention_pb_kernel(tc, h_attn, Wo, bo, out_0, out_1):
+    nc = tc.nc
+    o0 = out_0.flatten_outer_dims()
+    o1 = out_1.flatten_outer_dims()
+    hv = h_attn.rearrange("b (q jl) h d -> (b q) jl (h d)", jl=8)
+
+    with ExitStack() as ctx:
+        const = ctx.enter_context(tc.tile_pool(name="const", bufs=1))
+        keep = ctx.enter_context(tc.tile_pool(name="keep", bufs=1))
+        work = ctx.enter_context(tc.tile_pool(name="work", bufs=5))
+        psum = ctx.enter_context(tc.psum_pool(name="psum", bufs=1))
+        ctx.enter_context(tc.manual_schedule())
+
+        xraw = [keep.tile([P, 8, 512], BF16, name="xraw%d" % sg) for sg in range(2)]
+        wraw = [keep.tile([P, 4, N], BF16, name="wraw%d" % G) for G in range(2)]
+        brow = const.tile([P, N], BF16, name="brow")
+
+        def load_x(h0, h1):
+            nc.sync.dma_start(out=xraw[h0 // 8][:, :, (h0 % 8) * 64 : (h0 % 8) * 64 + (h1 - h0) * 64], in_=hv[:, :, h0 * 64 : h1 * 64])
+
+        def load_w(G, nh):
+            cols = slice(nh * NB, (nh + 1) * NB)
+            nc.sync.dma_start(out=wraw[G][:, :, cols], in_=Wo[G * 512 : (G + 1) * 512, cols].rearrange("(p t) n -> p t n", t=4))
+
+        nc.vector.memset(brow[:], 0.0)
+        load_w(0, 0)
+        nc.sync.dma_start(out=brow[0:1, :], in_=bo.rearrange("(o n) -> o n", o=1))
+        load_w(0, 1)
+        load_x(0, 8)
+        load_w(1, 0)
+        load_w(1, 1)
+        load_x(8, 16)
+        zero = const.tile([P, 1], F32, name="zero")
+        nc.gpsimd.memset(zero[:], 0.0)
+        warm = const.tile([P, 1], F32, name="warm")
+        nc.scalar.activation(out=warm[:], in_=zero[:], func=ACT.Identity, bias=zero[:, 0:1], scale=zero[:, 0:1])
+        ones = const.tile([P, P], BF16, name="ones")
+        nc.gpsimd.memset(ones[:], 1.0)
+        ident = const.tile([P, P], F32, name="ident")
+        make_identity(nc, ident[:])
+        perm = const.tile([P, P], F32, name="perm")
+        nc.vector.tensor_copy(
+            out=perm[:].rearrange("p (b jh g) -> p b jh g", b=4, jh=2),
+            in_=ident[:].rearrange("p (b g jh) -> p b jh g", b=4, jh=2),
+        )
+
+        x2 = [keep.tile([P, 4, 2, P], F32, name="x2_%d" % c) for c in range(4)]
+        yg = [keep.tile([P, 4096], BF16, name="yg%d" % sg, align_bytes=64) for sg in range(2)]
+        yc = [keep.tile([P, N], U32, name="yc%d" % sg, align_bytes=64) for sg in range(2)]
+        ys = [keep.tile([P, N], U8, name="ys%d" % sg, align_bytes=64) for sg in range(2)]
+        wg = [keep.tile([P, N, 4], BF16, name="wg%d" % G, align_bytes=64) for G in range(2)]
+        wc = keep.tile([P, 2, N], U32, name="wc", align_bytes=64)
+        ws = keep.tile([P, 2, N], U8, name="ws", align_bytes=64)
+        bias = keep.tile([P, N], F32, name="bias")
+
+        def make_bias():
+            for nh in range(2):
+                cols = slice(nh * NB, (nh + 1) * NB)
+                bp = psum.tile([P, NB], F32, name="acc", tag="acc", bufs=6)
+                nc.tensor.matmul(out=bp[:], lhsT=ones[:], rhs=brow[:, cols], start=True, stop=True)
+                nc.scalar.copy(out=bias[:, cols], in_=bp[:])
+
+        def warm_up(nh, times):
+            ps = psum.tile([P, NB], F32, name="acc", tag="acc", bufs=6)
+            for k in range(times):
+                nc.tensor.matmul(
+                    out=ps[:], lhsT=ones[:], rhs=wg[1][:, nh * NB : nh * NB + P, :].rearrange("p n t -> p (n t)"), start=True, stop=True
+                )
+
+        def reorder(c, on_vector):
+            xs = xraw[c // 2][:, :, (c % 2) * 256 : (c % 2 + 1) * 256]
+            xw = xs.bitcast(F32).rearrange("p jl (h d4 u) -> p u h jl d4", h=4, u=2)
+            for u in range(2):
+                dst = x2[c][:, :, u, :].rearrange("p h (jl d4) -> p h jl d4", jl=8)
+                if on_vector:
+                    nc.vector.tensor_copy(out=dst, in_=xw[:, u])
+                else:
+                    nc.scalar.copy(out=dst, in_=xw[:, u])
+
+        xts = {}
+
+        def transposes(hp):
+            xt = psum.tile([P, 4, P], F32, name="xt", tag="xt", bufs=2)
+            xts[hp] = xt
+            for hl in range(2):
+                h = 2 * hp + hl
+                for u in range(2):
+                    nc.tensor.transpose(out=xt[:, 2 * hl + u, :], in_=x2[h // 4][:, h % 4, u, :], identity=perm[:])
+
+        def copy_out(hp):
+            xt = xts[hp]
+            ygw = yg[hp // 4][:].bitcast(F32).rearrange("p (bj h g u) -> p bj h g u", bj=8, h=8, u=2)
+            h0 = (2 * hp) % 8
+            nc.scalar.copy(out=ygw[:, :, h0 : h0 + 2, :, :], in_=xt[:].rearrange("p (hl u) (bj g) -> p bj hl g u", u=2, bj=8))
+
+        def w_views(G, nh):
+            return wraw[G][:, :, nh * NB : (nh + 1) * NB].rearrange("p t n -> p n t"), wg[G][:, nh * NB : (nh + 1) * NB, :]
+
+        def w_inter_v(G, nh):
+            src, dst = w_views(G, nh)
+            nc.vector.tensor_copy(out=dst[:, 0:W_VEC, :], in_=src[:, 0:W_VEC, :])
+
+        def w_inter_s(G, nh):
+            src, dst = w_views(G, nh)
+            nc.scalar.copy(out=dst[:, W_VEC:NB, :], in_=src[:, W_VEC:NB, :])
+
+        def w_quant(G, nh):
+            cols = slice(nh * NB, (nh + 1) * NB)
+            nc.vector.quantize_mx(
+                out=wc[:, G, cols].bitcast(FP8X4), scales=ws[:, G, cols], in_=wg[G][:, cols, :].rearrange("p n t -> p (n t)")
+            )
+
+        def y_quant(sg):
+            nc.vector.quantize_mx(out=yc[sg][:].bitcast(FP8X4), scales=ys[sg][:], in_=yg[sg][:])
+
+        accs, ress, sts, facs, o8s = {}, {}, {}, {}, {}
+
+        def mm(i):
+            sg, b = i // 4, i % 4
+            for nh in range(2):
+                acc = psum.tile([P, NB], F32, name="acc", tag="acc", bufs=6)
+                accs[(i, nh)] = acc
+                cols = slice(nh * NB, (nh + 1) * NB)
+                for G in range(2):
+                    rows = slice((2 * b + G) * P, (2 * b + G + 1) * P)
+                    nc.tensor.matmul_mx(
+                        out=acc[:],
+                        lhsT=yc[sg][:, rows].bitcast(FP8X4),
+                        lhsT_scale=ys[sg][:, rows],
+                        rhs=wc[:, G, cols].bitcast(FP8X4),
+                        rhs_scale=ws[:, G, cols],
+                        start=(G == 0),
+                        stop=(G == 1),
+                    )
+
+        def res_of(i):
+            if i not in ress:
+                ress[i] = work.tile([P, N], F32, name="res", tag="res")
+            return ress[i]
+
+        def add(i, nh):
+            cols = slice(nh * NB, (nh + 1) * NB)
+            if (i, nh) not in BY_POOL:
+                nc.vector.tensor_tensor(out=res_of(i)[:, cols], in0=accs[(i, nh)][:], in1=bias[:, cols], op=ALU.add)
+
+        def pool_add(i, nh):
+            cols = slice(nh * NB, (nh + 1) * NB)
+            if (i, nh) in BY_POOL:
+                nc.scalar.copy(out=res_of(i)[:, cols], in_=accs[(i, nh)][:])
+                nc.gpsimd.tensor_tensor(out=res_of(i)[:, cols], in0=res_of(i)[:, cols], in1=bias[:, cols], op=ALU.add)
+
+        def absmax(i):
+            sts[i] = work.tile([P, 2], F32, name="st", tag="st")
+            nc.vector.tensor_reduce(out=sts[i][:, 0:1], in_=ress[i][:], axis=AX.X, op=ALU.max, apply_absolute_value=True)
+
+        def factor(i):
+            nc.vector.reciprocal(out=sts[i][:, 1:2], in_=sts[i][:, 0:1])
+            facs[i] = work.tile([P, 1], F32, name="fac", tag="fac")
+            nc.scalar.activation(out=facs[i][:], in_=sts[i][:, 1:2], func=ACT.Copy, scale=448.0)
+
+        def cast(i):
+            o8s[i] = work.tile([P, N], FP8, name="o8", tag="o8")
+            cv = LAST_VEC if i == TILES - 1 else 0
+            if cv:
+                nc.vector.tensor_scalar(
+                    out=o8s[i][:, 0:cv], in0=ress[i][:, 0:cv], scalar1=facs[i][:, 0:1], scalar2=None, op0=ALU.mult, saturate=False
+                )
+            nc.scalar.activation(
+                out=o8s[i][:, cv:N], in_=ress[i][:, cv:N], func=ACT.Identity, bias=zero[:, 0:1], scale=facs[i][:, 0:1], saturate=False
+            )
+
+        def row0(i):
+            return (i % 4) * 256 + (i // 4) * P
+
+        def store0(i):
+            nc.sync.dma_start(out=o0[row0(i) : row0(i) + P, :], in_=ress[i][:])
+
+        def store1(i):
+            nc.sync.dma_start(out=o1[row0(i) : row0(i) + P, :], in_=o8s[i][:].bitcast(U8))
+
+        w_inter_v(0, 0)
+        w_inter_s(0, 0)
+        w_inter_v(0, 1)
+        w_inter_s(0, 1)
+        make_bias()
+        w_quant(0, 0)
+        w_quant(0, 1)
+        reorder(0, True)
+        transposes(0)
+        transposes(1)
+        reorder(1, True)
+        copy_out(0)
+        copy_out(1)
+        transposes(2)
+        transposes(3)
+        w_inter_v(1, 0)
+        w_inter_s(1, 0)
+        copy_out(2)
+        copy_out(3)
+        w_inter_v(1, 1)
+        w_inter_s(1, 1)
+        warm_up(0, 4)
+        warm_up(1, 4)
+        w_quant(1, 0)
+        y_quant(0)
+        w_quant(1, 1)
+        mm(0)
+        mm(1)
+        mm(2)
+        reorder(2, False)
+        transposes(4)
+        transposes(5)
+        reorder(3, False)
+        copy_out(4)
+        copy_out(5)
+        transposes(6)
+        transposes(7)
+        copy_out(6)
+        copy_out(7)
+
+        waiting = []
+
+        def finish_waiting(between):
+            for k in waiting:
+                factor(k)
+            if between is not None:
+                pool_add(between, 1)
+            for k in waiting:
+                cast(k)
+                store1(k)
+            waiting.clear()
+
+        for s in range(TILES + 1):
+            if s < TILES:
+                add(s, 0)
+                if (s, 1) in BY_POOL:
+                    store0(s)
+                finish_waiting(s + 1 if s + 1 < TILES and s != Y1_STEP else None)
+            if s == Y1_STEP:
+                y_quant(1)
+                mm(4)
+            if s >= 1:
+                absmax(s - 1)
+                waiting.append(s - 1)
+            if s < TILES and (s, 1) not in BY_POOL:
+                add(s, 1)
+                store0(s)
+                finish_waiting(None)
+            if s + 3 < 4:
+                mm(s + 3)
+            if s >= Y1_STEP and s + 2 < TILES:
+                mm(s + 2)
+            if s == Y1_STEP:
+                pool_add(s + 1, 1)
+        finish_waiting(None)

@@ -20,9 +20,9 @@ NB = 512
 N = 1024
 TILES = 8
 W_VEC = 336
-LAST_VEC = 672
-BY_POOL = ((3, 1), (5, 1), (6, 1))
-Y1_STEP = 3
+VEC_CAST = {7: 672}
+EVAC_AT = {1: (1,), 2: (2,), 3: (3,), 4: (4, 5), 5: (6,), 6: (7,)}
+POOL_TILES = (1, 2, 3, 4, 5, 6, 7)
 
 
 def tile_reasoningmultiheadattention_pb_kernel(tc, h_attn, Wo, bo, out_0, out_1):
@@ -34,7 +34,7 @@ def tile_reasoningmultiheadattention_pb_kernel(tc, h_attn, Wo, bo, out_0, out_1)
     with ExitStack() as ctx:
         const = ctx.enter_context(tc.tile_pool(name="const", bufs=1))
         keep = ctx.enter_context(tc.tile_pool(name="keep", bufs=1))
-        work = ctx.enter_context(tc.tile_pool(name="work", bufs=5))
+        work = ctx.enter_context(tc.tile_pool(name="work", bufs=7))
         psum = ctx.enter_context(tc.psum_pool(name="psum", bufs=1))
         ctx.enter_context(tc.manual_schedule())
 
@@ -167,27 +167,30 @@ def tile_reasoningmultiheadattention_pb_kernel(tc, h_attn, Wo, bo, out_0, out_1)
 
         def add(i, nh):
             cols = slice(nh * NB, (nh + 1) * NB)
-            if (i, nh) not in BY_POOL:
-                nc.vector.tensor_tensor(out=res_of(i)[:, cols], in0=accs[(i, nh)][:], in1=bias[:, cols], op=ALU.add)
+            nc.vector.tensor_tensor(out=res_of(i)[:, cols], in0=accs[(i, nh)][:], in1=bias[:, cols], op=ALU.add)
+
+        def evac(i, nh):
+            cols = slice(nh * NB, (nh + 1) * NB)
+            nc.scalar.copy(out=res_of(i)[:, cols], in_=accs[(i, nh)][:])
 
         def pool_add(i, nh):
             cols = slice(nh * NB, (nh + 1) * NB)
-            if (i, nh) in BY_POOL:
-                nc.scalar.copy(out=res_of(i)[:, cols], in_=accs[(i, nh)][:])
-                nc.gpsimd.tensor_tensor(out=res_of(i)[:, cols], in0=res_of(i)[:, cols], in1=bias[:, cols], op=ALU.add)
+            nc.gpsimd.tensor_tensor(out=res_of(i)[:, cols], in0=res_of(i)[:, cols], in1=bias[:, cols], op=ALU.add)
 
         def absmax(i):
             sts[i] = work.tile([P, 2], F32, name="st", tag="st")
             nc.vector.tensor_reduce(out=sts[i][:, 0:1], in_=ress[i][:], axis=AX.X, op=ALU.max, apply_absolute_value=True)
 
-        def factor(i):
+        def recip(i):
             nc.vector.reciprocal(out=sts[i][:, 1:2], in_=sts[i][:, 0:1])
+
+        def factor(i):
             facs[i] = work.tile([P, 1], F32, name="fac", tag="fac")
             nc.scalar.activation(out=facs[i][:], in_=sts[i][:, 1:2], func=ACT.Copy, scale=448.0)
 
         def cast(i):
             o8s[i] = work.tile([P, N], FP8, name="o8", tag="o8")
-            cv = LAST_VEC if i == TILES - 1 else 0
+            cv = VEC_CAST.get(i, 0)
             if cv:
                 nc.vector.tensor_scalar(
                     out=o8s[i][:, 0:cv], in0=ress[i][:, 0:cv], scalar1=facs[i][:, 0:1], scalar2=None, op0=ALU.mult, saturate=False
@@ -226,6 +229,8 @@ def tile_reasoningmultiheadattention_pb_kernel(tc, h_attn, Wo, bo, out_0, out_1)
         copy_out(3)
         w_inter_v(1, 1)
         w_inter_s(1, 1)
+        reorder(2, False)
+        reorder(3, False)
         warm_up(0, 4)
         warm_up(1, 4)
         w_quant(1, 0)
@@ -233,50 +238,41 @@ def tile_reasoningmultiheadattention_pb_kernel(tc, h_attn, Wo, bo, out_0, out_1)
         w_quant(1, 1)
         mm(0)
         mm(1)
-        mm(2)
-        reorder(2, False)
         transposes(4)
         transposes(5)
-        reorder(3, False)
-        copy_out(4)
-        copy_out(5)
-        transposes(6)
-        transposes(7)
-        copy_out(6)
-        copy_out(7)
+        mm(2)
 
-        waiting = []
+        def by_pool(i):
+            evac(i, 1)
+            pool_add(i, 1)
 
-        def finish_waiting(between):
-            for k in waiting:
-                factor(k)
-            if between is not None:
-                pool_add(between, 1)
-            for k in waiting:
-                cast(k)
-                store1(k)
-            waiting.clear()
-
-        for s in range(TILES + 1):
+        for s in range(TILES + 2):
             if s < TILES:
                 add(s, 0)
-                if (s, 1) in BY_POOL:
-                    store0(s)
-                finish_waiting(s + 1 if s + 1 < TILES and s != Y1_STEP else None)
-            if s == Y1_STEP:
+                if s not in POOL_TILES:
+                    add(s, 1)
+                for i in EVAC_AT.get(s, ()):
+                    by_pool(i)
+                store0(s)
+            if s == 1:
+                copy_out(4)
+                copy_out(5)
+                transposes(6)
+                transposes(7)
+                mm(3)
+            if s == 2:
+                copy_out(6)
+                copy_out(7)
+            if s + 3 < TILES and s + 3 >= 6:
+                mm(s + 3)
+            if 0 <= s - 2:
+                recip(s - 2)
+                factor(s - 2)
+                cast(s - 2)
+                store1(s - 2)
+            if 1 <= s <= TILES:
+                absmax(s - 1)
+            if s == 2:
                 y_quant(1)
                 mm(4)
-            if s >= 1:
-                absmax(s - 1)
-                waiting.append(s - 1)
-            if s < TILES and (s, 1) not in BY_POOL:
-                add(s, 1)
-                store0(s)
-                finish_waiting(None)
-            if s + 3 < 4:
-                mm(s + 3)
-            if s >= Y1_STEP and s + 2 < TILES:
-                mm(s + 2)
-            if s == Y1_STEP:
-                pool_add(s + 1, 1)
-        finish_waiting(None)
+                mm(5)

@@ -120,16 +120,18 @@ def tile_reasoningmultiheadattention_pb_kernel(tc, h_attn, Wo, bo, out_0, out_1)
             h0 = (2 * hp) % 8
             nc.scalar.copy(out=ygw[:, :, h0 : h0 + 2, :, :], in_=xt[:].rearrange("p (hl u) (bj g) -> p bj hl g u", u=2, bj=8))
 
-        def w_views(G, nh):
-            return wraw[G][:, :, nh * NB : (nh + 1) * NB].rearrange("p t n -> p n t"), wg[G][:, nh * NB : (nh + 1) * NB, :]
+        def w_views(G, nh, c0, c1):
+            src = wraw[G][:, :, nh * NB + c0 : nh * NB + c1].rearrange("p t (c i) -> p c t i", i=4)
+            dst = wg[G][:, nh * NB + c0 : nh * NB + c1, :].rearrange("p (c i) t -> p c t i", i=4)
+            return src, dst
 
         def w_inter_v(G, nh):
-            src, dst = w_views(G, nh)
-            nc.vector.tensor_copy(out=dst[:, 0:W_VEC, :], in_=src[:, 0:W_VEC, :])
+            src, dst = w_views(G, nh, 0, W_VEC)
+            nc.vector.tensor_copy(out=dst, in_=src)
 
         def w_inter_s(G, nh):
-            src, dst = w_views(G, nh)
-            nc.scalar.copy(out=dst[:, W_VEC:NB, :], in_=src[:, W_VEC:NB, :])
+            src, dst = w_views(G, nh, W_VEC, NB)
+            nc.scalar.copy(out=dst, in_=src)
 
         def w_quant(G, nh):
             cols = slice(nh * NB, (nh + 1) * NB)

@@ -39,7 +39,7 @@ def tile_reasoningmultiheadattention_pb_kernel(tc, h_attn, Wo, bo, out_0, out_1)
         ctx.enter_context(tc.manual_schedule())
 
         xraw = [keep.tile([P, 8, 512], BF16, name="xraw%d" % sg) for sg in range(2)]
-        wraw = [keep.tile([P, 4, N], BF16, name="wraw%d" % G) for G in range(2)]
+        wraw = [[keep.tile([P, 4, NB], BF16, name="wraw%d%d" % (G, nh)) for nh in range(2)] for G in range(2)]
         brow = const.tile([P, N], BF16, name="brow")
 
         def load_x(h0, h1):
@@ -47,7 +47,7 @@ def tile_reasoningmultiheadattention_pb_kernel(tc, h_attn, Wo, bo, out_0, out_1)
 
         def load_w(G, nh):
             cols = slice(nh * NB, (nh + 1) * NB)
-            nc.sync.dma_start(out=wraw[G][:, :, cols], in_=Wo[G * 512 : (G + 1) * 512, cols].rearrange("(p t) n -> p t n", t=4))
+            nc.sync.dma_start(out=wraw[G][nh][:], in_=Wo[G * 512 : (G + 1) * 512, cols].rearrange("(p t) n -> p t n", t=4))
 
         nc.vector.memset(brow[:], 0.0)
         load_w(0, 0)
@@ -96,13 +96,12 @@ def tile_reasoningmultiheadattention_pb_kernel(tc, h_attn, Wo, bo, out_0, out_1)
 
         def reorder(c, on_vector):
             xs = xraw[c // 2][:, :, (c % 2) * 256 : (c % 2 + 1) * 256]
-            xw = xs.bitcast(F32).rearrange("p jl (h d4 u) -> p u h jl d4", h=4, u=2)
-            for u in range(2):
-                dst = x2[c][:, :, u, :].rearrange("p h (jl d4) -> p h jl d4", jl=8)
-                if on_vector:
-                    nc.vector.tensor_copy(out=dst, in_=xw[:, u])
-                else:
-                    nc.scalar.copy(out=dst, in_=xw[:, u])
+            src = xs.bitcast(F32).rearrange("p jl (h d4 u) -> p h u jl d4", h=4, u=2)
+            dst = x2[c][:].rearrange("p h u (jl d4) -> p h u jl d4", jl=8)
+            if on_vector:
+                nc.vector.tensor_copy(out=dst, in_=src)
+            else:
+                nc.scalar.copy(out=dst, in_=src)
 
         xts = {}
 
@@ -121,7 +120,7 @@ def tile_reasoningmultiheadattention_pb_kernel(tc, h_attn, Wo, bo, out_0, out_1)
             nc.scalar.copy(out=ygw[:, :, h0 : h0 + 2, :, :], in_=xt[:].rearrange("p (hl u) (bj g) -> p bj hl g u", u=2, bj=8))
 
         def w_views(G, nh, c0, c1):
-            src = wraw[G][:, :, nh * NB + c0 : nh * NB + c1].rearrange("p t (c i) -> p c t i", i=4)
+            src = wraw[G][nh][:, :, c0:c1].rearrange("p t (c i) -> p c t i", i=4)
             dst = wg[G][:, nh * NB + c0 : nh * NB + c1, :].rearrange("p (c i) t -> p c t i", i=4)
             return src, dst
 

@@ -21,7 +21,9 @@ N = 1024
 TILES = 8
 W_VEC = 336
 VEC_CAST = {7: 672}
-EVAC_AT = {1: (1,), 2: (2,), 3: (3,), 4: (4, 5), 5: (6,), 6: (7,)}
+EVAC_FIRST = {1: (1,), 2: (2,)}
+EVAC_MID = {3: (4,), 4: (5,), 5: (6,), 6: (7,)}
+EVAC_LAST = {2: (3,)}
 POOL_TILES = (1, 2, 3, 4, 5, 6, 7)
 
 
@@ -252,8 +254,14 @@ def tile_reasoningmultiheadattention_pb_kernel(tc, h_attn, Wo, bo, out_0, out_1)
                 add(s, 0)
                 if s not in POOL_TILES:
                     add(s, 1)
-                for i in EVAC_AT.get(s, ()):
+                for i in EVAC_FIRST.get(s, ()):
                     by_pool(i)
+            if 0 <= s - 2:
+                recip(s - 2)
+                factor(s - 2)
+            for i in EVAC_MID.get(s, ()):
+                by_pool(i)
+            if s < TILES:
                 store0(s)
             if s == 1:
                 copy_out(4)
@@ -267,10 +275,10 @@ def tile_reasoningmultiheadattention_pb_kernel(tc, h_attn, Wo, bo, out_0, out_1)
             if s + 3 < TILES and s + 3 >= 6:
                 mm(s + 3)
             if 0 <= s - 2:
-                recip(s - 2)
-                factor(s - 2)
                 cast(s - 2)
                 store1(s - 2)
+            for i in EVAC_LAST.get(s, ()):
+                by_pool(i)
             if 1 <= s <= TILES:
                 absmax(s - 1)
             if s == 2:

@@ -89,11 +89,11 @@ def tile_reasoningmultiheadattention_pb_kernel(tc, h_attn, Wo, bo, out_0, out_1)
                 nc.tensor.matmul(out=bp[:], lhsT=ones[:], rhs=brow[:, cols], start=True, stop=True)
                 nc.scalar.copy(out=bias[:, cols], in_=bp[:])
 
-        def warm_up(nh, times):
+        def warm_up(G, nh, times):
             ps = psum.tile([P, NB], F32, name="acc", tag="acc", bufs=6)
             for k in range(times):
                 nc.tensor.matmul(
-                    out=ps[:], lhsT=ones[:], rhs=wg[1][:, nh * NB : nh * NB + P, :].rearrange("p n t -> p (n t)"), start=True, stop=True
+                    out=ps[:], lhsT=ones[:], rhs=wg[G][:, nh * NB : nh * NB + P, :].rearrange("p n t -> p (n t)"), start=True, stop=True
                 )
 
         def reorder(c, on_vector):
@@ -218,9 +218,11 @@ def tile_reasoningmultiheadattention_pb_kernel(tc, h_attn, Wo, bo, out_0, out_1)
         make_bias()
         w_quant(0, 0)
         w_quant(0, 1)
+        warm_up(0, 1, 3)
         reorder(0, True)
         transposes(0)
         transposes(1)
+        warm_up(0, 1, 1)
         reorder(1, True)
         copy_out(0)
         copy_out(1)
@@ -234,8 +236,8 @@ def tile_reasoningmultiheadattention_pb_kernel(tc, h_attn, Wo, bo, out_0, out_1)
         w_inter_s(1, 1)
         reorder(2, False)
         reorder(3, False)
-        warm_up(0, 4)
-        warm_up(1, 4)
+        warm_up(1, 0, 3)
+        warm_up(1, 1, 3)
         w_quant(1, 0)
         y_quant(0)
         w_quant(1, 1)

@@ -96,6 +96,20 @@ def tile_reasoningmultiheadattention_pb_kernel(tc, h_attn, Wo, bo, out_0, out_1)
                     out=ps[:], lhsT=ones[:], rhs=wg[G][:, nh * NB : nh * NB + P, :].rearrange("p n t -> p (n t)"), start=True, stop=True
                 )
 
+        def hold(G, nh, times):
+            ps = psum.tile([P, NB], F32, name="xt", tag="xt", bufs=2)
+            cols = slice(nh * NB, (nh + 1) * NB)
+            for k in range(times):
+                nc.tensor.matmul_mx(
+                    out=ps[:],
+                    lhsT=wc[:, G, nh * NB : nh * NB + P].bitcast(FP8X4),
+                    lhsT_scale=ws[:, G, nh * NB : nh * NB + P],
+                    rhs=wc[:, G, cols].bitcast(FP8X4),
+                    rhs_scale=ws[:, G, cols],
+                    start=True,
+                    stop=True,
+                )
+
         def reorder(c, on_vector):
             xs = xraw[c // 2][:, :, (c % 2) * 256 : (c % 2 + 1) * 256]
             src = xs.bitcast(F32).rearrange("p jl (h d4 u) -> p h u jl d4", h=4, u=2)
@@ -216,13 +230,14 @@ def tile_reasoningmultiheadattention_pb_kernel(tc, h_attn, Wo, bo, out_0, out_1)
         w_inter_v(0, 1)
         w_inter_s(0, 1)
         make_bias()
+        warm_up(0, 1, 2)
         w_quant(0, 0)
         w_quant(0, 1)
-        warm_up(0, 1, 3)
+        hold(0, 1, 2)
         reorder(0, True)
         transposes(0)
         transposes(1)
-        warm_up(0, 1, 1)
+        warm_up(0, 1, 2)
         reorder(1, True)
         copy_out(0)
         copy_out(1)
@@ -239,6 +254,7 @@ def tile_reasoningmultiheadattention_pb_kernel(tc, h_attn, Wo, bo, out_0, out_1)
         warm_up(1, 0, 3)
         warm_up(1, 1, 3)
         w_quant(1, 0)
+        hold(1, 0, 2)
         y_quant(0)
         w_quant(1, 1)
         mm(0)
@@ -273,7 +289,9 @@ def tile_reasoningmultiheadattention_pb_kernel(tc, h_attn, Wo, bo, out_0, out_1)
                 mm(3)
             if s == 2:
                 copy_out(6)
+                hold(0, 0, 2)
                 copy_out(7)
+                hold(0, 1, 3)
             if s + 3 < TILES and s + 3 >= 6:
                 mm(s + 3)
             if 0 <= s - 2:

@@ -22,8 +22,8 @@ TILES = 8
 W_VEC = 336
 VEC_CAST = {7: 672}
 EVAC_FIRST = {1: (1,), 2: (2,)}
-EVAC_MID = {3: (4,), 4: (5,), 5: (6,), 6: (7,)}
-EVAC_LAST = {2: (3,)}
+EVAC_MID = {4: (5,), 5: (6,), 6: (7,)}
+EVAC_LAST = {2: (3,), 3: (4,)}
 POOL_TILES = (1, 2, 3, 4, 5, 6, 7)
 
 
@@ -277,6 +277,10 @@ def tile_reasoningmultiheadattention_pb_kernel(tc, h_attn, Wo, bo, out_0, out_1)
             if 0 <= s - 2:
                 recip(s - 2)
                 factor(s - 2)
+            if s == 3:
+                y_quant(1)
+                mm(4)
+                mm(5)
             for i in EVAC_MID.get(s, ()):
                 by_pool(i)
             if s < TILES:
@@ -301,7 +305,3 @@ def tile_reasoningmultiheadattention_pb_kernel(tc, h_attn, Wo, bo, out_0, out_1)
                 by_pool(i)
             if 1 <= s <= TILES:
                 absmax(s - 1)
-            if s == 2:
-                y_quant(1)
-                mm(4)
-                mm(5)

@@ -41,7 +41,9 @@ def tile_reasoningmultiheadattention_pb_kernel(tc, h_attn, Wo, bo, out_0, out_1)
         ctx.enter_context(tc.manual_schedule())
 
         xraw = [keep.tile([P, 8, 512], BF16, name="xraw%d" % sg) for sg in range(2)]
+        wfull = [keep.tile([P, 4, N], BF16, name="wfull%d" % G) for G in range(2)]
         wraw = [[keep.tile([P, 4, NB], BF16, name="wraw%d%d" % (G, nh)) for nh in range(2)] for G in range(2)]
+        WHOLE = (0,)
         brow = const.tile([P, N], BF16, name="brow")
 
         def load_x(h0, h1):
@@ -49,7 +51,11 @@ def tile_reasoningmultiheadattention_pb_kernel(tc, h_attn, Wo, bo, out_0, out_1)
 
         def load_w(G, nh):
             cols = slice(nh * NB, (nh + 1) * NB)
-            nc.sync.dma_start(out=wraw[G][nh][:], in_=Wo[G * 512 : (G + 1) * 512, cols].rearrange("(p t) n -> p t n", t=4))
+            if G in WHOLE:
+                if nh == 0:
+                    nc.sync.dma_start(out=wfull[G][:].rearrange("p t n -> p (t n)"), in_=Wo[G * 512 : (G + 1) * 512, :].rearrange("(p t) n -> p (t n)", t=4))
+            else:
+                nc.sync.dma_start(out=wraw[G][nh][:], in_=Wo[G * 512 : (G + 1) * 512, cols].rearrange("(p t) n -> p t n", t=4))
 
         nc.vector.memset(brow[:], 0.0)
         load_w(0, 0)
@@ -136,7 +142,7 @@ def tile_reasoningmultiheadattention_pb_kernel(tc, h_attn, Wo, bo, out_0, out_1)
             nc.scalar.copy(out=ygw[:, :, h0 : h0 + 2, :, :], in_=xt[:].rearrange("p (hl u) (bj g) -> p bj hl g u", u=2, bj=8))
 
         def w_views(G, nh, c0, c1):
-            src = wraw[G][nh][:, :, c0:c1].rearrange("p t (c i) -> p c t i", i=4)
+            src = (wfull[G][:, :, nh * NB + c0 : nh * NB + c1] if G in WHOLE else wraw[G][nh][:, :, c0:c1]).rearrange("p t (c i) -> p c t i", i=4)
             dst = wg[G][:, nh * NB + c0 : nh * NB + c1, :].rearrange("p (c i) t -> p c t i", i=4)
             return src, dst
 
@@ -232,13 +238,13 @@ def tile_reasoningmultiheadattention_pb_kernel(tc, h_attn, Wo, bo, out_0, out_1)
         make_bias()
         warm_up(0, 1, 2)
         w_quant(0, 0)
-        w_quant(0, 1)
-        hold(0, 1, 2)
+        hold(0, 0, 2)
         reorder(0, True)
         transposes(0)
         transposes(1)
         warm_up(0, 1, 2)
         reorder(1, True)
+        w_quant(0, 1)
         copy_out(0)
         copy_out(1)
         transposes(2)

@@ -16,15 +16,17 @@ ACT = mybir.ActivationFunctionType
 AX = mybir.AxisListType
 
 P = 128
-NB = 512
 N = 1024
+NB = 512
+K_PASS = 512
 TILES = 8
+ACC_BANKS = 6
+XT_BANKS = 2
+RES_BUFS = 7
 W_VEC = 336
-VEC_CAST = {7: 672}
-EVAC_FIRST = {1: (1,), 2: (2,)}
-EVAC_MID = {4: (5,), 5: (6,), 6: (7,)}
-EVAC_LAST = {2: (3,), 3: (4,)}
-POOL_TILES = (1, 2, 3, 4, 5, 6, 7)
+LAST_VEC = 672
+AHEAD_FROM = 3
+BETWEEN_FROM = 5
 
 
 def tile_reasoningmultiheadattention_pb_kernel(tc, h_attn, Wo, bo, out_0, out_1):
@@ -36,35 +38,28 @@ def tile_reasoningmultiheadattention_pb_kernel(tc, h_attn, Wo, bo, out_0, out_1)
     with ExitStack() as ctx:
         const = ctx.enter_context(tc.tile_pool(name="const", bufs=1))
         keep = ctx.enter_context(tc.tile_pool(name="keep", bufs=1))
-        work = ctx.enter_context(tc.tile_pool(name="work", bufs=7))
+        work = ctx.enter_context(tc.tile_pool(name="work", bufs=RES_BUFS))
         psum = ctx.enter_context(tc.psum_pool(name="psum", bufs=1))
         ctx.enter_context(tc.manual_schedule())
 
         xraw = [keep.tile([P, 8, 512], BF16, name="xraw%d" % sg) for sg in range(2)]
-        wfull = [keep.tile([P, 4, N], BF16, name="wfull%d" % G) for G in range(2)]
-        wraw = [[keep.tile([P, 4, NB], BF16, name="wraw%d%d" % (G, nh)) for nh in range(2)] for G in range(2)]
-        WHOLE = (0,)
+        wraw0 = keep.tile([P, 4, N], BF16, name="wraw0")
+        wraw1 = [keep.tile([P, 4, NB], BF16, name="wraw1%d" % nh) for nh in range(2)]
         brow = const.tile([P, N], BF16, name="brow")
 
-        def load_x(h0, h1):
-            nc.sync.dma_start(out=xraw[h0 // 8][:, :, (h0 % 8) * 64 : (h0 % 8) * 64 + (h1 - h0) * 64], in_=hv[:, :, h0 * 64 : h1 * 64])
-
-        def load_w(G, nh):
-            cols = slice(nh * NB, (nh + 1) * NB)
-            if G in WHOLE:
-                if nh == 0:
-                    nc.sync.dma_start(out=wfull[G][:].rearrange("p t n -> p (t n)"), in_=Wo[G * 512 : (G + 1) * 512, :].rearrange("(p t) n -> p (t n)", t=4))
-            else:
-                nc.sync.dma_start(out=wraw[G][nh][:], in_=Wo[G * 512 : (G + 1) * 512, cols].rearrange("(p t) n -> p t n", t=4))
+        def load_x(sg):
+            nc.sync.dma_start(out=xraw[sg][:], in_=hv[:, :, sg * 512 : (sg + 1) * 512])
 
         nc.vector.memset(brow[:], 0.0)
-        load_w(0, 0)
+        nc.sync.dma_start(out=wraw0[:].rearrange("p t n -> p (t n)"), in_=Wo[0:K_PASS, :].rearrange("(p t) n -> p (t n)", t=4))
         nc.sync.dma_start(out=brow[0:1, :], in_=bo.rearrange("(o n) -> o n", o=1))
-        load_w(0, 1)
-        load_x(0, 8)
-        load_w(1, 0)
-        load_w(1, 1)
-        load_x(8, 16)
+        load_x(0)
+        for nh in range(2):
+            nc.sync.dma_start(
+                out=wraw1[nh][:], in_=Wo[K_PASS : 2 * K_PASS, nh * NB : (nh + 1) * NB].rearrange("(p t) n -> p t n", t=4)
+            )
+        load_x(1)
+
         zero = const.tile([P, 1], F32, name="zero")
         nc.gpsimd.memset(zero[:], 0.0)
         warm = const.tile([P, 1], F32, name="warm")
@@ -88,22 +83,25 @@ def tile_reasoningmultiheadattention_pb_kernel(tc, h_attn, Wo, bo, out_0, out_1)
         ws = keep.tile([P, 2, N], U8, name="ws", align_bytes=64)
         bias = keep.tile([P, N], F32, name="bias")
 
+        def acc_bank():
+            return psum.tile([P, NB], F32, name="acc", tag="acc", bufs=ACC_BANKS)
+
         def make_bias():
             for nh in range(2):
                 cols = slice(nh * NB, (nh + 1) * NB)
-                bp = psum.tile([P, NB], F32, name="acc", tag="acc", bufs=6)
+                bp = acc_bank()
                 nc.tensor.matmul(out=bp[:], lhsT=ones[:], rhs=brow[:, cols], start=True, stop=True)
                 nc.scalar.copy(out=bias[:, cols], in_=bp[:])
 
-        def warm_up(G, nh, times):
-            ps = psum.tile([P, NB], F32, name="acc", tag="acc", bufs=6)
+        def idle_plain(G, nh, times):
+            ps = acc_bank()
             for k in range(times):
                 nc.tensor.matmul(
                     out=ps[:], lhsT=ones[:], rhs=wg[G][:, nh * NB : nh * NB + P, :].rearrange("p n t -> p (n t)"), start=True, stop=True
                 )
 
-        def hold(G, nh, times):
-            ps = psum.tile([P, NB], F32, name="xt", tag="xt", bufs=2)
+        def idle_mx(G, nh, times):
+            ps = psum.tile([P, NB], F32, name="xt", tag="xt", bufs=XT_BANKS)
             cols = slice(nh * NB, (nh + 1) * NB)
             for k in range(times):
                 nc.tensor.matmul_mx(
@@ -116,7 +114,7 @@ def tile_reasoningmultiheadattention_pb_kernel(tc, h_attn, Wo, bo, out_0, out_1)
                     stop=True,
                 )
 
-        def reorder(c, on_vector):
+        def gather_words(c, on_vector):
             xs = xraw[c // 2][:, :, (c % 2) * 256 : (c % 2 + 1) * 256]
             src = xs.bitcast(F32).rearrange("p jl (h d4 u) -> p h u jl d4", h=4, u=2)
             dst = x2[c][:].rearrange("p h u (jl d4) -> p h u jl d4", jl=8)
@@ -128,7 +126,7 @@ def tile_reasoningmultiheadattention_pb_kernel(tc, h_attn, Wo, bo, out_0, out_1)
         xts = {}
 
         def transposes(hp):
-            xt = psum.tile([P, 4, P], F32, name="xt", tag="xt", bufs=2)
+            xt = psum.tile([P, 4, P], F32, name="xt", tag="xt", bufs=XT_BANKS)
             xts[hp] = xt
             for hl in range(2):
                 h = 2 * hp + hl
@@ -136,21 +134,22 @@ def tile_reasoningmultiheadattention_pb_kernel(tc, h_attn, Wo, bo, out_0, out_1)
                     nc.tensor.transpose(out=xt[:, 2 * hl + u, :], in_=x2[h // 4][:, h % 4, u, :], identity=perm[:])
 
         def copy_out(hp):
-            xt = xts[hp]
             ygw = yg[hp // 4][:].bitcast(F32).rearrange("p (bj h g u) -> p bj h g u", bj=8, h=8, u=2)
             h0 = (2 * hp) % 8
-            nc.scalar.copy(out=ygw[:, :, h0 : h0 + 2, :, :], in_=xt[:].rearrange("p (hl u) (bj g) -> p bj hl g u", u=2, bj=8))
+            nc.scalar.copy(out=ygw[:, :, h0 : h0 + 2, :, :], in_=xts[hp][:].rearrange("p (hl u) (bj g) -> p bj hl g u", u=2, bj=8))
+
+        def y_quant(sg):
+            nc.vector.quantize_mx(out=yc[sg][:].bitcast(FP8X4), scales=ys[sg][:], in_=yg[sg][:])
 
         def w_views(G, nh, c0, c1):
-            src = (wfull[G][:, :, nh * NB + c0 : nh * NB + c1] if G in WHOLE else wraw[G][nh][:, :, c0:c1]).rearrange("p t (c i) -> p c t i", i=4)
+            raw = wraw0[:, :, nh * NB + c0 : nh * NB + c1] if G == 0 else wraw1[nh][:, :, c0:c1]
+            src = raw.rearrange("p t (c i) -> p c t i", i=4)
             dst = wg[G][:, nh * NB + c0 : nh * NB + c1, :].rearrange("p (c i) t -> p c t i", i=4)
             return src, dst
 
-        def w_inter_v(G, nh):
+        def interleave(G, nh):
             src, dst = w_views(G, nh, 0, W_VEC)
             nc.vector.tensor_copy(out=dst, in_=src)
-
-        def w_inter_s(G, nh):
             src, dst = w_views(G, nh, W_VEC, NB)
             nc.scalar.copy(out=dst, in_=src)
 
@@ -160,15 +159,12 @@ def tile_reasoningmultiheadattention_pb_kernel(tc, h_attn, Wo, bo, out_0, out_1)
                 out=wc[:, G, cols].bitcast(FP8X4), scales=ws[:, G, cols], in_=wg[G][:, cols, :].rearrange("p n t -> p (n t)")
             )
 
-        def y_quant(sg):
-            nc.vector.quantize_mx(out=yc[sg][:].bitcast(FP8X4), scales=ys[sg][:], in_=yg[sg][:])
-
         accs, ress, sts, facs, o8s = {}, {}, {}, {}, {}
 
         def mm(i):
             sg, b = i // 4, i % 4
             for nh in range(2):
-                acc = psum.tile([P, NB], F32, name="acc", tag="acc", bufs=6)
+                acc = acc_bank()
                 accs[(i, nh)] = acc
                 cols = slice(nh * NB, (nh + 1) * NB)
                 for G in range(2):
@@ -192,28 +188,23 @@ def tile_reasoningmultiheadattention_pb_kernel(tc, h_attn, Wo, bo, out_0, out_1)
             cols = slice(nh * NB, (nh + 1) * NB)
             nc.vector.tensor_tensor(out=res_of(i)[:, cols], in0=accs[(i, nh)][:], in1=bias[:, cols], op=ALU.add)
 
-        def evac(i, nh):
-            cols = slice(nh * NB, (nh + 1) * NB)
-            nc.scalar.copy(out=res_of(i)[:, cols], in_=accs[(i, nh)][:])
-
-        def pool_add(i, nh):
-            cols = slice(nh * NB, (nh + 1) * NB)
+        def add_by_pool(i):
+            cols = slice(NB, N)
+            nc.scalar.copy(out=res_of(i)[:, cols], in_=accs[(i, 1)][:])
             nc.gpsimd.tensor_tensor(out=res_of(i)[:, cols], in0=res_of(i)[:, cols], in1=bias[:, cols], op=ALU.add)
 
         def absmax(i):
             sts[i] = work.tile([P, 2], F32, name="st", tag="st")
             nc.vector.tensor_reduce(out=sts[i][:, 0:1], in_=ress[i][:], axis=AX.X, op=ALU.max, apply_absolute_value=True)
 
-        def recip(i):
-            nc.vector.reciprocal(out=sts[i][:, 1:2], in_=sts[i][:, 0:1])
-
         def factor(i):
+            nc.vector.reciprocal(out=sts[i][:, 1:2], in_=sts[i][:, 0:1])
             facs[i] = work.tile([P, 1], F32, name="fac", tag="fac")
             nc.scalar.activation(out=facs[i][:], in_=sts[i][:, 1:2], func=ACT.Copy, scale=448.0)
 
         def cast(i):
             o8s[i] = work.tile([P, N], FP8, name="o8", tag="o8")
-            cv = VEC_CAST.get(i, 0)
+            cv = LAST_VEC if i == TILES - 1 else 0
             if cv:
                 nc.vector.tensor_scalar(
                     out=o8s[i][:, 0:cv], in0=ress[i][:, 0:cv], scalar1=facs[i][:, 0:1], scalar2=None, op0=ALU.mult, saturate=False
@@ -231,36 +222,32 @@ def tile_reasoningmultiheadattention_pb_kernel(tc, h_attn, Wo, bo, out_0, out_1)
         def store1(i):
             nc.sync.dma_start(out=o1[row0(i) : row0(i) + P, :], in_=o8s[i][:].bitcast(U8))
 
-        w_inter_v(0, 0)
-        w_inter_s(0, 0)
-        w_inter_v(0, 1)
-        w_inter_s(0, 1)
+        interleave(0, 0)
+        interleave(0, 1)
         make_bias()
-        warm_up(0, 1, 2)
+        idle_plain(0, 1, 2)
         w_quant(0, 0)
-        hold(0, 0, 2)
-        reorder(0, True)
+        idle_mx(0, 0, 2)
+        gather_words(0, True)
         transposes(0)
         transposes(1)
-        warm_up(0, 1, 2)
-        reorder(1, True)
+        idle_plain(0, 1, 2)
+        gather_words(1, True)
         w_quant(0, 1)
         copy_out(0)
         copy_out(1)
         transposes(2)
         transposes(3)
-        w_inter_v(1, 0)
-        w_inter_s(1, 0)
+        interleave(1, 0)
         copy_out(2)
         copy_out(3)
-        w_inter_v(1, 1)
-        w_inter_s(1, 1)
-        reorder(2, False)
-        reorder(3, False)
-        warm_up(1, 0, 3)
-        warm_up(1, 1, 3)
+        interleave(1, 1)
+        gather_words(2, False)
+        gather_words(3, False)
+        idle_plain(1, 0, 3)
+        idle_plain(1, 1, 3)
         w_quant(1, 0)
-        hold(1, 0, 2)
+        idle_mx(1, 0, 2)
         y_quant(0)
         w_quant(1, 1)
         mm(0)
@@ -269,26 +256,21 @@ def tile_reasoningmultiheadattention_pb_kernel(tc, h_attn, Wo, bo, out_0, out_1)
         transposes(5)
         mm(2)
 
-        def by_pool(i):
-            evac(i, 1)
-            pool_add(i, 1)
-
         for s in range(TILES + 2):
             if s < TILES:
                 add(s, 0)
-                if s not in POOL_TILES:
-                    add(s, 1)
-                for i in EVAC_FIRST.get(s, ()):
-                    by_pool(i)
-            if 0 <= s - 2:
-                recip(s - 2)
+            if s == 0:
+                add(s, 1)
+            if 1 <= s < AHEAD_FROM:
+                add_by_pool(s)
+            if s >= 2:
                 factor(s - 2)
             if s == 3:
                 y_quant(1)
                 mm(4)
                 mm(5)
-            for i in EVAC_MID.get(s, ()):
-                by_pool(i)
+            if BETWEEN_FROM <= s + 1 < TILES:
+                add_by_pool(s + 1)
             if s < TILES:
                 store0(s)
             if s == 1:
@@ -299,15 +281,15 @@ def tile_reasoningmultiheadattention_pb_kernel(tc, h_attn, Wo, bo, out_0, out_1)
                 mm(3)
             if s == 2:
                 copy_out(6)
-                hold(0, 0, 2)
+                idle_mx(0, 0, 2)
                 copy_out(7)
-                hold(0, 1, 3)
-            if s + 3 < TILES and s + 3 >= 6:
+                idle_mx(0, 1, 3)
+            if 6 <= s + 3 < TILES:
                 mm(s + 3)
-            if 0 <= s - 2:
+            if s >= 2:
                 cast(s - 2)
                 store1(s - 2)
-            for i in EVAC_LAST.get(s, ()):
-                by_pool(i)
+            if AHEAD_FROM <= s + 1 < BETWEEN_FROM:
+                add_by_pool(s + 1)
             if 1 <= s <= TILES:
                 absmax(s - 1)

@@ -23,7 +23,7 @@ TILES = 8
 ACC_BANKS = 6
 XT_BANKS = 2
 RES_BUFS = 7
-W_VEC = 336
+W_VEC = ((336, 336), (432, 336))
 LAST_VEC = 672
 AHEAD_FROM = 3
 BETWEEN_FROM = 5
@@ -119,7 +119,8 @@ def tile_reasoningmultiheadattention_pb_kernel(tc, h_attn, Wo, bo, out_0, out_1)
             src = xs.bitcast(F32).rearrange("p jl (h d4 u) -> p h u jl d4", h=4, u=2)
             dst = x2[c][:].rearrange("p h u (jl d4) -> p h u jl d4", jl=8)
             if on_vector:
-                nc.vector.tensor_copy(out=dst, in_=src)
+                for hh in range(2):
+                    nc.vector.tensor_copy(out=dst[:, 2 * hh : 2 * hh + 2], in_=src[:, 2 * hh : 2 * hh + 2])
             else:
                 nc.scalar.copy(out=dst, in_=src)
 
@@ -148,9 +149,9 @@ def tile_reasoningmultiheadattention_pb_kernel(tc, h_attn, Wo, bo, out_0, out_1)
             return src, dst
 
         def interleave(G, nh):
-            src, dst = w_views(G, nh, 0, W_VEC)
+            src, dst = w_views(G, nh, 0, W_VEC[G][nh])
             nc.vector.tensor_copy(out=dst, in_=src)
-            src, dst = w_views(G, nh, W_VEC, NB)
+            src, dst = w_views(G, nh, W_VEC[G][nh], NB)
             nc.scalar.copy(out=dst, in_=src)
 
         def w_quant(G, nh):
@@ -200,7 +201,10 @@ def tile_reasoningmultiheadattention_pb_kernel(tc, h_attn, Wo, bo, out_0, out_1)
         def factor(i):
             nc.vector.reciprocal(out=sts[i][:, 1:2], in_=sts[i][:, 0:1])
             facs[i] = work.tile([P, 1], F32, name="fac", tag="fac")
-            nc.scalar.activation(out=facs[i][:], in_=sts[i][:, 1:2], func=ACT.Copy, scale=448.0)
+            if i == TILES - 1:
+                nc.vector.tensor_scalar(out=facs[i][:], in0=sts[i][:, 1:2], scalar1=448.0, scalar2=None, op0=ALU.mult)
+            else:
+                nc.scalar.activation(out=facs[i][:], in_=sts[i][:, 1:2], func=ACT.Copy, scale=448.0)
 
         def cast(i):
             o8s[i] = work.tile([P, N], FP8, name="o8", tag="o8")
@@ -225,9 +229,8 @@ def tile_reasoningmultiheadattention_pb_kernel(tc, h_attn, Wo, bo, out_0, out_1)
         interleave(0, 0)
         interleave(0, 1)
         make_bias()
-        idle_plain(0, 1, 2)
+        idle_plain(0, 1, 3)
         w_quant(0, 0)
-        idle_mx(0, 0, 2)
         gather_words(0, True)
         transposes(0)
         transposes(1)
@@ -245,7 +248,7 @@ def tile_reasoningmultiheadattention_pb_kernel(tc, h_attn, Wo, bo, out_0, out_1)
         gather_words(2, False)
         gather_words(3, False)
         idle_plain(1, 0, 3)
-        idle_plain(1, 1, 3)
+        idle_plain(1, 1, 2)
         w_quant(1, 0)
         idle_mx(1, 0, 2)
         y_quant(0)

@@ -20,11 +20,11 @@ N = 1024
 NB = 512
 K_PASS = 512
 TILES = 8
-ACC_BANKS = 6
-XT_BANKS = 2
+ACC_BANKS = 4
+XT_BANKS = 4
 RES_BUFS = 7
 W_VEC = ((336, 336), (432, 336))
-LAST_VEC = 672
+LAST_VEC = 704
 AHEAD_FROM = 3
 BETWEEN_FROM = 5
 
@@ -234,21 +234,20 @@ def tile_reasoningmultiheadattention_pb_kernel(tc, h_attn, Wo, bo, out_0, out_1)
         gather_words(0, True)
         transposes(0)
         transposes(1)
-        idle_plain(0, 1, 2)
         gather_words(1, True)
+        transposes(2)
+        transposes(3)
         w_quant(0, 1)
         copy_out(0)
         copy_out(1)
-        transposes(2)
-        transposes(3)
         interleave(1, 0)
         copy_out(2)
         copy_out(3)
         interleave(1, 1)
         gather_words(2, False)
         gather_words(3, False)
-        idle_plain(1, 0, 3)
-        idle_plain(1, 1, 2)
+        idle_plain(1, 0, 4)
+        idle_plain(1, 1, 3)
         w_quant(1, 0)
         idle_mx(1, 0, 2)
         y_quant(0)
@@ -257,7 +256,6 @@ def tile_reasoningmultiheadattention_pb_kernel(tc, h_attn, Wo, bo, out_0, out_1)
         mm(1)
         transposes(4)
         transposes(5)
-        mm(2)
 
         for s in range(TILES + 2):
             if s < TILES:
@@ -287,8 +285,8 @@ def tile_reasoningmultiheadattention_pb_kernel(tc, h_attn, Wo, bo, out_0, out_1)
                 idle_mx(0, 0, 2)
                 copy_out(7)
                 idle_mx(0, 1, 3)
-            if 6 <= s + 3 < TILES:
-                mm(s + 3)
+            if s + 2 in (2, 6, 7):
+                mm(s + 2)
             if s >= 2:
                 cast(s - 2)
                 store1(s - 2)

@@ -139,8 +139,9 @@ def tile_reasoningmultiheadattention_pb_kernel(tc, h_attn, Wo, bo, out_0, out_1)
             h0 = (2 * hp) % 8
             nc.scalar.copy(out=ygw[:, :, h0 : h0 + 2, :, :], in_=xts[hp][:].rearrange("p (hl u) (bj g) -> p bj hl g u", u=2, bj=8))
 
-        def y_quant(sg):
-            nc.vector.quantize_mx(out=yc[sg][:].bitcast(FP8X4), scales=ys[sg][:], in_=yg[sg][:])
+        def y_quant(sg, b0=0, nb=4):
+            w = slice(b0 * 256, (b0 + nb) * 256)
+            nc.vector.quantize_mx(out=yc[sg][:, w].bitcast(FP8X4), scales=ys[sg][:, w], in_=yg[sg][:, b0 * N : (b0 + nb) * N])
 
         def w_views(G, nh, c0, c1):
             raw = wraw0[:, :, nh * NB + c0 : nh * NB + c1] if G == 0 else wraw1[nh][:, :, c0:c1]
@@ -162,9 +163,9 @@ def tile_reasoningmultiheadattention_pb_kernel(tc, h_attn, Wo, bo, out_0, out_1)
 
         accs, ress, sts, facs, o8s = {}, {}, {}, {}, {}
 
-        def mm(i):
+        def mm(i, halves=(0, 1)):
             sg, b = i // 4, i % 4
-            for nh in range(2):
+            for nh in halves:
                 acc = acc_bank()
                 accs[(i, nh)] = acc
                 cols = slice(nh * NB, (nh + 1) * NB)
@@ -246,21 +247,25 @@ def tile_reasoningmultiheadattention_pb_kernel(tc, h_attn, Wo, bo, out_0, out_1)
         interleave(1, 1)
         gather_words(2, False)
         gather_words(3, False)
-        idle_plain(1, 0, 4)
-        idle_plain(1, 1, 3)
+        idle_plain(1, 0, 3)
+        idle_plain(1, 1, 2)
         w_quant(1, 0)
-        idle_mx(1, 0, 2)
-        y_quant(0)
+        y_quant(0, 0, 1)
+        y_quant(0, 1, 1)
+        y_quant(0, 2, 2)
         w_quant(1, 1)
-        mm(0)
-        mm(1)
+        mm(0, (0,))
+        mm(1, (0,))
+        mm(0, (1,))
+        mm(1, (1,))
         transposes(4)
         transposes(5)
 
         for s in range(TILES + 2):
-            if s < TILES:
+            if s < TILES and s != 1:
                 add(s, 0)
             if s == 0:
+                add(1, 0)
                 add(s, 1)
             if 1 <= s < AHEAD_FROM:
                 add_by_pool(s)

@@ -272,9 +272,11 @@ def tile_reasoningmultiheadattention_pb_kernel(tc, h_attn, Wo, bo, out_0, out_1)
             if s >= 2:
                 factor(s - 2)
             if s == 3:
-                y_quant(1)
+                y_quant(1, 0, 1)
                 mm(4)
+                y_quant(1, 1, 1)
                 mm(5)
+                y_quant(1, 2, 2)
             if BETWEEN_FROM <= s + 1 < TILES:
                 add_by_pool(s + 1)
             if s < TILES:

from contextlib import ExitStack

import concourse.mybir as mybir
from concourse.masks import make_identity

FLOPS = 2 * 1024 * 1024 * 1024

F32 = mybir.dt.float32
BF16 = mybir.dt.bfloat16
U32 = mybir.dt.uint32
U8 = mybir.dt.uint8
FP8X4 = mybir.dt.float8_e4m3fn_x4
FP8 = mybir.dt.float8_e4m3fn
ALU = mybir.AluOpType
ACT = mybir.ActivationFunctionType
AX = mybir.AxisListType

P = 128
N = 1024
NB = 512
K_PASS = 512
TILES = 8
ACC_BANKS = 4
XT_BANKS = 4
RES_BUFS = 7
W_VEC = ((336, 336), (432, 336))
LAST_VEC = 704
AHEAD_FROM = 3
BETWEEN_FROM = 5


def tile_reasoningmultiheadattention_pb_kernel(tc, h_attn, Wo, bo, out_0, out_1):
    nc = tc.nc
    o0 = out_0.flatten_outer_dims()
    o1 = out_1.flatten_outer_dims()
    hv = h_attn.rearrange("b (q jl) h d -> (b q) jl (h d)", jl=8)

    with ExitStack() as ctx:
        const = ctx.enter_context(tc.tile_pool(name="const", bufs=1))
        keep = ctx.enter_context(tc.tile_pool(name="keep", bufs=1))
        work = ctx.enter_context(tc.tile_pool(name="work", bufs=RES_BUFS))
        psum = ctx.enter_context(tc.psum_pool(name="psum", bufs=1))
        ctx.enter_context(tc.manual_schedule())

        xraw = [keep.tile([P, 8, 512], BF16, name="xraw%d" % sg) for sg in range(2)]
        wraw0 = keep.tile([P, 4, N], BF16, name="wraw0")
        wraw1 = [keep.tile([P, 4, NB], BF16, name="wraw1%d" % nh) for nh in range(2)]
        brow = const.tile([P, N], BF16, name="brow")

        def load_x(sg):
            nc.sync.dma_start(out=xraw[sg][:], in_=hv[:, :, sg * 512 : (sg + 1) * 512])

        nc.vector.memset(brow[:], 0.0)
        nc.sync.dma_start(out=wraw0[:].rearrange("p t n -> p (t n)"), in_=Wo[0:K_PASS, :].rearrange("(p t) n -> p (t n)", t=4))
        nc.sync.dma_start(out=brow[0:1, :], in_=bo.rearrange("(o n) -> o n", o=1))
        load_x(0)
        for nh in range(2):
            nc.sync.dma_start(
                out=wraw1[nh][:], in_=Wo[K_PASS : 2 * K_PASS, nh * NB : (nh + 1) * NB].rearrange("(p t) n -> p t n", t=4)
            )
        load_x(1)

        zero = const.tile([P, 1], F32, name="zero")
        nc.gpsimd.memset(zero[:], 0.0)
        warm = const.tile([P, 1], F32, name="warm")
        nc.scalar.activation(out=warm[:], in_=zero[:], func=ACT.Identity, bias=zero[:, 0:1], scale=zero[:, 0:1])
        ones = const.tile([P, P], BF16, name="ones")
        nc.gpsimd.memset(ones[:], 1.0)
        ident = const.tile([P, P], F32, name="ident")
        make_identity(nc, ident[:])
        perm = const.tile([P, P], F32, name="perm")
        nc.vector.tensor_copy(
            out=perm[:].rearrange("p (b jh g) -> p b jh g", b=4, jh=2),
            in_=ident[:].rearrange("p (b g jh) -> p b jh g", b=4, jh=2),
        )

        x2 = [keep.tile([P, 4, 2, P], F32, name="x2_%d" % c) for c in range(4)]
        yg = [keep.tile([P, 4096], BF16, name="yg%d" % sg, align_bytes=64) for sg in range(2)]
        yc = [keep.tile([P, N], U32, name="yc%d" % sg, align_bytes=64) for sg in range(2)]
        ys = [keep.tile([P, N], U8, name="ys%d" % sg, align_bytes=64) for sg in range(2)]
        wg = [keep.tile([P, N, 4], BF16, name="wg%d" % G, align_bytes=64) for G in range(2)]
        wc = keep.tile([P, 2, N], U32, name="wc", align_bytes=64)
        ws = keep.tile([P, 2, N], U8, name="ws", align_bytes=64)
        bias = keep.tile([P, N], F32, name="bias")

        def acc_bank():
            return psum.tile([P, NB], F32, name="acc", tag="acc", bufs=ACC_BANKS)

        def make_bias():
            for nh in range(2):
                cols = slice(nh * NB, (nh + 1) * NB)
                bp = acc_bank()
                nc.tensor.matmul(out=bp[:], lhsT=ones[:], rhs=brow[:, cols], start=True, stop=True)
                nc.scalar.copy(out=bias[:, cols], in_=bp[:])

        def idle_plain(G, nh, times):
            ps = acc_bank()
            for k in range(times):
                nc.tensor.matmul(
                    out=ps[:], lhsT=ones[:], rhs=wg[G][:, nh * NB : nh * NB + P, :].rearrange("p n t -> p (n t)"), start=True, stop=True
                )

        def idle_mx(G, nh, times):
            ps = psum.tile([P, NB], F32, name="xt", tag="xt", bufs=XT_BANKS)
            cols = slice(nh * NB, (nh + 1) * NB)
            for k in range(times):
                nc.tensor.matmul_mx(
                    out=ps[:],
                    lhsT=wc[:, G, nh * NB : nh * NB + P].bitcast(FP8X4),
                    lhsT_scale=ws[:, G, nh * NB : nh * NB + P],
                    rhs=wc[:, G, cols].bitcast(FP8X4),
                    rhs_scale=ws[:, G, cols],
                    start=True,
                    stop=True,
                )

        def gather_words(c, on_vector):
            xs = xraw[c // 2][:, :, (c % 2) * 256 : (c % 2 + 1) * 256]
            src = xs.bitcast(F32).rearrange("p jl (h d4 u) -> p h u jl d4", h=4, u=2)
            dst = x2[c][:].rearrange("p h u (jl d4) -> p h u jl d4", jl=8)
            if on_vector:
                for hh in range(2):
                    nc.vector.tensor_copy(out=dst[:, 2 * hh : 2 * hh + 2], in_=src[:, 2 * hh : 2 * hh + 2])
            else:
                nc.scalar.copy(out=dst, in_=src)

        xts = {}

        def transposes(hp):
            xt = psum.tile([P, 4, P], F32, name="xt", tag="xt", bufs=XT_BANKS)
            xts[hp] = xt
            for hl in range(2):
                h = 2 * hp + hl
                for u in range(2):
                    nc.tensor.transpose(out=xt[:, 2 * hl + u, :], in_=x2[h // 4][:, h % 4, u, :], identity=perm[:])

        def copy_out(hp):
            ygw = yg[hp // 4][:].bitcast(F32).rearrange("p (bj h g u) -> p bj h g u", bj=8, h=8, u=2)
            h0 = (2 * hp) % 8
            nc.scalar.copy(out=ygw[:, :, h0 : h0 + 2, :, :], in_=xts[hp][:].rearrange("p (hl u) (bj g) -> p bj hl g u", u=2, bj=8))

        def y_quant(sg, b0=0, nb=4):
            w = slice(b0 * 256, (b0 + nb) * 256)
            nc.vector.quantize_mx(out=yc[sg][:, w].bitcast(FP8X4), scales=ys[sg][:, w], in_=yg[sg][:, b0 * N : (b0 + nb) * N])

        def w_views(G, nh, c0, c1):
            raw = wraw0[:, :, nh * NB + c0 : nh * NB + c1] if G == 0 else wraw1[nh][:, :, c0:c1]
            src = raw.rearrange("p t (c i) -> p c t i", i=4)
            dst = wg[G][:, nh * NB + c0 : nh * NB + c1, :].rearrange("p (c i) t -> p c t i", i=4)
            return src, dst

        def interleave(G, nh):
            src, dst = w_views(G, nh, 0, W_VEC[G][nh])
            nc.vector.tensor_copy(out=dst, in_=src)
            src, dst = w_views(G, nh, W_VEC[G][nh], NB)
            nc.scalar.copy(out=dst, in_=src)

        def w_quant(G, nh):
            cols = slice(nh * NB, (nh + 1) * NB)
            nc.vector.quantize_mx(
                out=wc[:, G, cols].bitcast(FP8X4), scales=ws[:, G, cols], in_=wg[G][:, cols, :].rearrange("p n t -> p (n t)")
            )

        accs, ress, sts, facs, o8s = {}, {}, {}, {}, {}

        def mm(i, halves=(0, 1)):
            sg, b = i // 4, i % 4
            for nh in halves:
                acc = acc_bank()
                accs[(i, nh)] = acc
                cols = slice(nh * NB, (nh + 1) * NB)
                for G in range(2):
                    rows = slice((2 * b + G) * P, (2 * b + G + 1) * P)
                    nc.tensor.matmul_mx(
                        out=acc[:],
                        lhsT=yc[sg][:, rows].bitcast(FP8X4),
                        lhsT_scale=ys[sg][:, rows],
                        rhs=wc[:, G, cols].bitcast(FP8X4),
                        rhs_scale=ws[:, G, cols],
                        start=(G == 0),
                        stop=(G == 1),
                    )

        def res_of(i):
            if i not in ress:
                ress[i] = work.tile([P, N], F32, name="res", tag="res")
            return ress[i]

        def add(i, nh):
            cols = slice(nh * NB, (nh + 1) * NB)
            nc.vector.tensor_tensor(out=res_of(i)[:, cols], in0=accs[(i, nh)][:], in1=bias[:, cols], op=ALU.add)

        def add_by_pool(i):
            cols = slice(NB, N)
            nc.scalar.copy(out=res_of(i)[:, cols], in_=accs[(i, 1)][:])
            nc.gpsimd.tensor_tensor(out=res_of(i)[:, cols], in0=res_of(i)[:, cols], in1=bias[:, cols], op=ALU.add)

        def absmax(i):
            sts[i] = work.tile([P, 2], F32, name="st", tag="st")
            nc.vector.tensor_reduce(out=sts[i][:, 0:1], in_=ress[i][:], axis=AX.X, op=ALU.max, apply_absolute_value=True)

        def factor(i):
            nc.vector.reciprocal(out=sts[i][:, 1:2], in_=sts[i][:, 0:1])
            facs[i] = work.tile([P, 1], F32, name="fac", tag="fac")
            if i == TILES - 1:
                nc.vector.tensor_scalar(out=facs[i][:], in0=sts[i][:, 1:2], scalar1=448.0, scalar2=None, op0=ALU.mult)
            else:
                nc.scalar.activation(out=facs[i][:], in_=sts[i][:, 1:2], func=ACT.Copy, scale=448.0)

        def cast(i):
            o8s[i] = work.tile([P, N], FP8, name="o8", tag="o8")
            cv = LAST_VEC if i == TILES - 1 else 0
            if cv:
                nc.vector.tensor_scalar(
                    out=o8s[i][:, 0:cv], in0=ress[i][:, 0:cv], scalar1=facs[i][:, 0:1], scalar2=None, op0=ALU.mult, saturate=False
                )
            nc.scalar.activation(
                out=o8s[i][:, cv:N], in_=ress[i][:, cv:N], func=ACT.Identity, bias=zero[:, 0:1], scale=facs[i][:, 0:1], saturate=False
            )

        def row0(i):
            return (i % 4) * 256 + (i // 4) * P

        def store0(i):
            nc.sync.dma_start(out=o0[row0(i) : row0(i) + P, :], in_=ress[i][:])

        def store1(i):
            nc.sync.dma_start(out=o1[row0(i) : row0(i) + P, :], in_=o8s[i][:].bitcast(U8))

        interleave(0, 0)
        interleave(0, 1)
        make_bias()
        idle_plain(0, 1, 3)
        w_quant(0, 0)
        gather_words(0, True)
        transposes(0)
        transposes(1)
        gather_words(1, True)
        transposes(2)
        transposes(3)
        w_quant(0, 1)
        copy_out(0)
        copy_out(1)
        interleave(1, 0)
        copy_out(2)
        copy_out(3)
        interleave(1, 1)
        gather_words(2, False)
        gather_words(3, False)
        idle_plain(1, 0, 3)
        idle_plain(1, 1, 2)
        w_quant(1, 0)
        y_quant(0, 0, 1)
        y_quant(0, 1, 1)
        y_quant(0, 2, 2)
        w_quant(1, 1)
        mm(0, (0,))
        mm(1, (0,))
        mm(0, (1,))
        mm(1, (1,))
        transposes(4)
        transposes(5)

        for s in range(TILES + 2):
            if s < TILES and s != 1:
                add(s, 0)
            if s == 0:
                add(1, 0)
                add(s, 1)
            if 1 <= s < AHEAD_FROM:
                add_by_pool(s)
            if s >= 2:
                factor(s - 2)
            if s == 3:
                y_quant(1, 0, 1)
                mm(4)
                y_quant(1, 1, 1)
                mm(5)
                y_quant(1, 2, 2)
            if BETWEEN_FROM <= s + 1 < TILES:
                add_by_pool(s + 1)
            if s < TILES:
                store0(s)
            if s == 1:
                copy_out(4)
                copy_out(5)
                transposes(6)
                transposes(7)
                mm(3)
            if s == 2:
                copy_out(6)
                idle_mx(0, 0, 2)
                copy_out(7)
                idle_mx(0, 1, 3)
            if s + 2 in (2, 6, 7):
                mm(s + 2)
            if s >= 2:
                cast(s - 2)
                store1(s - 2)
            if AHEAD_FROM <= s + 1 < BETWEEN_FROM:
                add_by_pool(s + 1)
            if 1 <= s <= TILES:
                absmax(s - 1)
